import numpy as np
import ml_dtypes

BF16 = ml_dtypes.bfloat16


def bf(x):
    return np.asarray(x, np.float32).astype(BF16)


def f32(x):
    return np.asarray(x, np.float32)


def f64(x):
    return np.asarray(x).astype(np.float64)


def striped(idx):
    return np.tile(idx.reshape(-1, 16).T, (8, 1))


S, D, M, N, CA, CB, CC = 512, 128, 128, 128, 9, 5, 2


def make_lap():
    sizes = np.tile(np.array([CA, CB, CC]), N // (CA + CB + CC))
    label = np.repeat(np.arange(sizes.size), sizes)[np.random.permutation(N)]
    adj = (label[:, None] == label[None, :]).astype(np.float64) - np.eye(N)
    return -adj / adj.sum(axis=1, keepdims=True)


def setup_inputs():
    return {"table": bf(np.random.standard_normal((S, D))), "lap": bf(make_lap()), "w0": bf(np.random.standard_normal((D, M)) / np.sqrt(D)), "w1": bf(np.random.standard_normal((D, M)) / np.sqrt(D)), "w2": bf(np.random.standard_normal((D, M)) / np.sqrt(D)), "b": f32(0.1 * np.random.standard_normal((M, 1))), "offs": striped(np.random.permutation(np.tile(np.arange(S), 2))[:N])}


def reference(table, lap, w0, w1, w2, b, offs):
    idx = offs[:16].T.reshape(-1)
    x = f64(table)[idx].T
    y0 = f64(w0).T @ x
    y1 = f64(w1).T @ x
    y2 = f64(w2).T @ x
    z = y1 + 2.0 * (y2 @ f64(lap))
    return np.maximum(y0 - y2 + z @ f64(lap) + f64(b), 0.0)

@@ -1,0 +1,78 @@
+import concourse.mybir as mybir
+from concourse.masks import make_identity
+
+P = 128
+S = 512
+BLOCKS = S // P
+N = 128
+HALF = N // 2
+BF16, F32, U16 = mybir.dt.bfloat16, mybir.dt.float32, mybir.dt.uint16
+MULT, ADD, MAX = mybir.AluOpType.mult, mybir.AluOpType.add, mybir.AluOpType.max
+
+FLOPS = 2 * P * P * N * 5
+
+
+def tile_gcndeno_kernel(tc, table, lap, w0, w1, w2, b, offs, out):
+    nc = tc.nc
+    with tc.tile_pool(name="held", bufs=1) as held, tc.psum_pool(name="psum", bufs=1) as psum:
+        rows = held.tile([P, BLOCKS, P], BF16, name="rows")
+        nc.sync.dma_start(rows[:], table.rearrange("(n p) d -> p n d", p=P))
+        offsets = held.tile([P, N // 16], U16, name="offsets")
+        nc.sync.dma_start(offsets[:], offs)
+        w2_sb = held.tile([P, P], BF16, name="w2_sb")
+        nc.scalar.dma_start(w2_sb[:], w2)
+        w1_sb = held.tile([P, P], BF16, name="w1_sb")
+        nc.scalar.dma_start(w1_sb[:], w1)
+        w0_sb = held.tile([P, P], BF16, name="w0_sb")
+        nc.scalar.dma_start(w0_sb[:], w0)
+        lap_sb = held.tile([P, P], BF16, name="lap_sb")
+        nc.sync.dma_start(lap_sb[:], lap)
+        bias = held.tile([P, 1], F32, name="bias")
+        nc.sync.dma_start(bias[:], b)
+
+        ident_bf = held.tile([P, P], BF16, name="ident_bf")
+        make_identity(nc, ident_bf[:])
+        ident_f32 = held.tile([P, P], F32, name="ident_f32")
+        make_identity(nc, ident_f32[:])
+        w2_neg = held.tile([P, P], BF16, name="w2_neg")
+        nc.vector.tensor_scalar(w2_neg[:], w2_sb[:], -1.0, None, MULT)
+
+        window_ps = psum.tile([P, S], BF16, name="window_ps")
+        for n in range(BLOCKS):
+            nc.tensor.transpose(window_ps[:, n * P : (n + 1) * P], rows[:, n, :], ident_bf[:])
+        window = held.tile([P, S], BF16, name="window")
+        nc.vector.tensor_copy(window[:], window_ps[:])
+
+        y2_ps = psum.tile([P, N], F32, name="y2_ps")
+        nc.tensor.matmul(y2_ps[:], w2_sb[:], window[:].indirect(offsets[:]), start=True, stop=True)
+        y1_ps = psum.tile([P, N], F32, name="y1_ps")
+        nc.tensor.matmul(y1_ps[:], w1_sb[:], window[:].indirect(offsets[:]), start=True, stop=True)
+        acc_ps = psum.tile([P, N], F32, name="acc_ps")
+        nc.tensor.matmul(acc_ps[:], w0_sb[:], window[:].indirect(offsets[:]), start=True, stop=False)
+        for h in range(2):
+            nc.tensor.matmul(
+                acc_ps[:, h * HALF : (h + 1) * HALF],
+                w2_neg[:],
+                window[:].indirect(offsets[:, h * (HALF // 16) : (h + 1) * (HALF // 16)]),
+                start=False,
+                stop=False,
+            )
+
+        y2x2 = held.tile([P, N], BF16, name="y2x2")
+        nc.vector.tensor_scalar(y2x2[:], y2_ps[:], 2.0, None, MULT)
+        y1_sb = held.tile([P, N], F32, name="y1_sb")
+        nc.scalar.copy(y1_sb[:], y1_ps[:])
+        y2x2T_ps = psum.tile([N, P], BF16, name="y2x2T_ps")
+        nc.tensor.transpose(y2x2T_ps[:], y2x2[:], ident_bf[:])
+        y2x2T = held.tile([N, P], BF16, name="y2x2T")
+        nc.vector.tensor_copy(y2x2T[:], y2x2T_ps[:])
+        zT_ps = psum.tile([N, P], F32, name="zT_ps")
+        nc.tensor.matmul(zT_ps[:], y1_sb[:], ident_f32[:], is_transpose=True, start=True, stop=False)
+        nc.tensor.matmul(zT_ps[:], lap_sb[:], y2x2T[:], start=False, stop=True)
+        zT = held.tile([N, P], BF16, name="zT")
+        nc.vector.tensor_copy(zT[:], zT_ps[:])
+
+        nc.tensor.matmul(acc_ps[:], zT[:], lap_sb[:], start=False, stop=True)
+        result = held.tile([P, N], F32, name="result")
+        nc.vector.tensor_scalar(result[:], acc_ps[:], bias[:, 0:1], 0.0, ADD, MAX)
+        nc.sync.dma_start(out, result[:])

@@ -14,9 +14,15 @@ FLOPS = 2 * P * P * N * 5
 
 def tile_gcndeno_kernel(tc, table, lap, w0, w1, w2, b, offs, out):
     nc = tc.nc
-    with tc.tile_pool(name="held", bufs=1) as held, tc.psum_pool(name="psum", bufs=1) as psum:
-        rows = held.tile([P, BLOCKS, P], BF16, name="rows")
-        nc.sync.dma_start(rows[:], table.rearrange("(n p) d -> p n d", p=P))
+    with (
+        tc.tile_pool(name="held", bufs=1) as held,
+        tc.psum_pool(name="psum", bufs=1) as psum,
+        tc.psum_pool(name="flips", bufs=BLOCKS) as flips,
+    ):
+        rows = [held.tile([P, P], BF16, name=f"rows{n}") for n in range(BLOCKS)]
+        for n in range(BLOCKS):
+            queue = nc.sync if n % 2 == 0 else nc.scalar
+            queue.dma_start(rows[n][:], table[n * P : (n + 1) * P, :])
         offsets = held.tile([P, N // 16], U16, name="offsets")
         nc.sync.dma_start(offsets[:], offs)
         w2_sb = held.tile([P, P], BF16, name="w2_sb")
@@ -37,11 +43,14 @@ def tile_gcndeno_kernel(tc, table, lap, w0, w1, w2, b, offs, out):
         w2_neg = held.tile([P, P], BF16, name="w2_neg")
         nc.vector.tensor_scalar(w2_neg[:], w2_sb[:], -1.0, None, MULT)
 
-        window_ps = psum.tile([P, S], BF16, name="window_ps")
-        for n in range(BLOCKS):
-            nc.tensor.transpose(window_ps[:, n * P : (n + 1) * P], rows[:, n, :], ident_bf[:])
         window = held.tile([P, S], BF16, name="window")
-        nc.vector.tensor_copy(window[:], window_ps[:])
+        for n in range(BLOCKS):
+            flipped = flips.tile([P, P], BF16, name="flipped")
+            nc.tensor.transpose(flipped[:], rows[n][:], ident_bf[:])
+            if n % 2 == 0:
+                nc.vector.tensor_copy(window[:, n * P : (n + 1) * P], flipped[:])
+            else:
+                nc.scalar.copy(window[:, n * P : (n + 1) * P], flipped[:])
 
         y2_ps = psum.tile([P, N], F32, name="y2_ps")
         nc.tensor.matmul(y2_ps[:], w2_sb[:], window[:].indirect(offsets[:]), start=True, stop=True)
@@ -62,10 +71,10 @@ def tile_gcndeno_kernel(tc, table, lap, w0, w1, w2, b, offs, out):
         nc.vector.tensor_scalar(y2x2[:], y2_ps[:], 2.0, None, MULT)
         y1_sb = held.tile([P, N], F32, name="y1_sb")
         nc.scalar.copy(y1_sb[:], y1_ps[:])
-        y2x2T_ps = psum.tile([N, P], BF16, name="y2x2T_ps")
-        nc.tensor.transpose(y2x2T_ps[:], y2x2[:], ident_bf[:])
+        flipped = flips.tile([N, P], BF16, name="flipped")
+        nc.tensor.transpose(flipped[:], y2x2[:], ident_bf[:])
         y2x2T = held.tile([N, P], BF16, name="y2x2T")
-        nc.vector.tensor_copy(y2x2T[:], y2x2T_ps[:])
+        nc.vector.tensor_copy(y2x2T[:], flipped[:])
         zT_ps = psum.tile([N, P], F32, name="zT_ps")
         nc.tensor.matmul(zT_ps[:], y1_sb[:], ident_f32[:], is_transpose=True, start=True, stop=False)
         nc.tensor.matmul(zT_ps[:], lap_sb[:], y2x2T[:], start=False, stop=True)

@@ -41,23 +41,37 @@ def tile_gcndeno_kernel(tc, table, lap, w0, w1, w2, b, offs, out):
         ident_f32 = held.tile([P, P], F32, name="ident_f32")
         make_identity(nc, ident_f32[:])
         w2_neg = held.tile([P, P], BF16, name="w2_neg")
-        nc.vector.tensor_scalar(w2_neg[:], w2_sb[:], -1.0, None, MULT)
+        nc.gpsimd.tensor_scalar(w2_neg[:], w2_sb[:], -1.0, None, MULT)
 
         window = held.tile([P, S], BF16, name="window")
         for n in range(BLOCKS):
             flipped = flips.tile([P, P], BF16, name="flipped")
             nc.tensor.transpose(flipped[:], rows[n][:], ident_bf[:])
-            if n % 2 == 0:
-                nc.vector.tensor_copy(window[:, n * P : (n + 1) * P], flipped[:])
-            else:
-                nc.scalar.copy(window[:, n * P : (n + 1) * P], flipped[:])
+            nc.vector.tensor_copy(window[:, n * P : (n + 1) * P], flipped[:])
 
+        looked_up = window[:].indirect(offsets[:])
         y2_ps = psum.tile([P, N], F32, name="y2_ps")
-        nc.tensor.matmul(y2_ps[:], w2_sb[:], window[:].indirect(offsets[:]), start=True, stop=True)
+        nc.tensor.matmul(y2_ps[:], w2_sb[:], looked_up, start=True, stop=True)
+        y2x2 = held.tile([P, N], BF16, name="y2x2")
+        nc.vector.tensor_scalar(y2x2[:], y2_ps[:], 2.0, None, MULT)
+
         y1_ps = psum.tile([P, N], F32, name="y1_ps")
-        nc.tensor.matmul(y1_ps[:], w1_sb[:], window[:].indirect(offsets[:]), start=True, stop=True)
+        nc.tensor.matmul(y1_ps[:], w1_sb[:], looked_up, start=True, stop=True)
+        y1_sb = held.tile([P, N], F32, name="y1_sb")
+        nc.vector.tensor_copy(y1_sb[:], y1_ps[:])
+
+        flipped = flips.tile([N, P], BF16, name="flipped")
+        nc.tensor.transpose(flipped[:], y2x2[:], ident_bf[:])
+        y2x2T = held.tile([N, P], BF16, name="y2x2T")
+        nc.vector.tensor_copy(y2x2T[:], flipped[:])
+
+        zT_ps = psum.tile([N, P], F32, name="zT_ps")
+        nc.tensor.matmul(zT_ps[:], y1_sb[:], ident_f32[:], is_transpose=True, start=True, stop=False)
         acc_ps = psum.tile([P, N], F32, name="acc_ps")
-        nc.tensor.matmul(acc_ps[:], w0_sb[:], window[:].indirect(offsets[:]), start=True, stop=False)
+        nc.tensor.matmul(acc_ps[:], w0_sb[:], looked_up, start=True, stop=False)
+        nc.tensor.matmul(zT_ps[:], lap_sb[:], y2x2T[:], start=False, stop=True)
+        zT = held.tile([N, P], BF16, name="zT")
+        nc.vector.tensor_copy(zT[:], zT_ps[:])
         for h in range(2):
             nc.tensor.matmul(
                 acc_ps[:, h * HALF : (h + 1) * HALF],
@@ -66,20 +80,6 @@ def tile_gcndeno_kernel(tc, table, lap, w0, w1, w2, b, offs, out):
                 start=False,
                 stop=False,
             )
-
-        y2x2 = held.tile([P, N], BF16, name="y2x2")
-        nc.vector.tensor_scalar(y2x2[:], y2_ps[:], 2.0, None, MULT)
-        y1_sb = held.tile([P, N], F32, name="y1_sb")
-        nc.scalar.copy(y1_sb[:], y1_ps[:])
-        flipped = flips.tile([N, P], BF16, name="flipped")
-        nc.tensor.transpose(flipped[:], y2x2[:], ident_bf[:])
-        y2x2T = held.tile([N, P], BF16, name="y2x2T")
-        nc.vector.tensor_copy(y2x2T[:], flipped[:])
-        zT_ps = psum.tile([N, P], F32, name="zT_ps")
-        nc.tensor.matmul(zT_ps[:], y1_sb[:], ident_f32[:], is_transpose=True, start=True, stop=False)
-        nc.tensor.matmul(zT_ps[:], lap_sb[:], y2x2T[:], start=False, stop=True)
-        zT = held.tile([N, P], BF16, name="zT")
-        nc.vector.tensor_copy(zT[:], zT_ps[:])
 
         nc.tensor.matmul(acc_ps[:], zT[:], lap_sb[:], start=False, stop=True)
         result = held.tile([P, N], F32, name="result")

@@ -6,6 +6,7 @@ S = 512
 BLOCKS = S // P
 N = 128
 HALF = N // 2
+WARM_UP = 16
 BF16, F32, U16 = mybir.dt.bfloat16, mybir.dt.float32, mybir.dt.uint16
 MULT, ADD, MAX = mybir.AluOpType.mult, mybir.AluOpType.add, mybir.AluOpType.max
 
@@ -17,8 +18,14 @@ def tile_gcndeno_kernel(tc, table, lap, w0, w1, w2, b, offs, out):
     with (
         tc.tile_pool(name="held", bufs=1) as held,
         tc.psum_pool(name="psum", bufs=1) as psum,
-        tc.psum_pool(name="flips", bufs=BLOCKS) as flips,
+        tc.psum_pool(name="flips", bufs=3) as flips,
     ):
+        zeros = held.tile([P, P], BF16, name="zeros")
+        nc.vector.memset(zeros[:], 0.0)
+        warm_ps = psum.tile([P, P], F32, name="warm_ps")
+        for k in range(WARM_UP):
+            nc.tensor.matmul(warm_ps[:], zeros[:], zeros[:], start=True, stop=True)
+
         rows = [held.tile([P, P], BF16, name=f"rows{n}") for n in range(BLOCKS)]
         for n in range(BLOCKS):
             queue = nc.sync if n % 2 == 0 else nc.scalar

@@ -6,7 +6,6 @@ S = 512
 BLOCKS = S // P
 N = 128
 HALF = N // 2
-WARM_UP = 16
 BF16, F32, U16 = mybir.dt.bfloat16, mybir.dt.float32, mybir.dt.uint16
 MULT, ADD, MAX = mybir.AluOpType.mult, mybir.AluOpType.add, mybir.AluOpType.max
 
@@ -18,14 +17,8 @@ def tile_gcndeno_kernel(tc, table, lap, w0, w1, w2, b, offs, out):
     with (
         tc.tile_pool(name="held", bufs=1) as held,
         tc.psum_pool(name="psum", bufs=1) as psum,
-        tc.psum_pool(name="flips", bufs=3) as flips,
+        tc.psum_pool(name="flips", bufs=BLOCKS) as flips,
     ):
-        zeros = held.tile([P, P], BF16, name="zeros")
-        nc.vector.memset(zeros[:], 0.0)
-        warm_ps = psum.tile([P, P], F32, name="warm_ps")
-        for k in range(WARM_UP):
-            nc.tensor.matmul(warm_ps[:], zeros[:], zeros[:], start=True, stop=True)
-
         rows = [held.tile([P, P], BF16, name=f"rows{n}") for n in range(BLOCKS)]
         for n in range(BLOCKS):
             queue = nc.sync if n % 2 == 0 else nc.scalar
@@ -44,11 +37,12 @@ def tile_gcndeno_kernel(tc, table, lap, w0, w1, w2, b, offs, out):
         nc.sync.dma_start(bias[:], b)
 
         ident_bf = held.tile([P, P], BF16, name="ident_bf")
-        make_identity(nc, ident_bf[:])
+        nc.vector.memset(ident_bf[:], 0.0)
+        make_identity(nc, ident_bf[:], nomemset=True)
         ident_f32 = held.tile([P, P], F32, name="ident_f32")
-        make_identity(nc, ident_f32[:])
+        nc.vector.tensor_copy(ident_f32[:], ident_bf[:])
         w2_neg = held.tile([P, P], BF16, name="w2_neg")
-        nc.gpsimd.tensor_scalar(w2_neg[:], w2_sb[:], -1.0, None, MULT)
+        nc.vector.tensor_scalar(w2_neg[:], w2_sb[:], -1.0, None, MULT)
 
         window = held.tile([P, S], BF16, name="window")
         for n in range(BLOCKS):

@@ -5,9 +5,8 @@ P = 128
 S = 512
 BLOCKS = S // P
 N = 128
-HALF = N // 2
 BF16, F32, U16 = mybir.dt.bfloat16, mybir.dt.float32, mybir.dt.uint16
-MULT, ADD, MAX = mybir.AluOpType.mult, mybir.AluOpType.add, mybir.AluOpType.max
+MULT, ADD, SUBTRACT = mybir.AluOpType.mult, mybir.AluOpType.add, mybir.AluOpType.subtract
 
 FLOPS = 2 * P * P * N * 5
 
@@ -37,12 +36,9 @@ def tile_gcndeno_kernel(tc, table, lap, w0, w1, w2, b, offs, out):
         nc.sync.dma_start(bias[:], b)
 
         ident_bf = held.tile([P, P], BF16, name="ident_bf")
-        nc.vector.memset(ident_bf[:], 0.0)
-        make_identity(nc, ident_bf[:], nomemset=True)
+        make_identity(nc, ident_bf[:])
         ident_f32 = held.tile([P, P], F32, name="ident_f32")
-        nc.vector.tensor_copy(ident_f32[:], ident_bf[:])
-        w2_neg = held.tile([P, P], BF16, name="w2_neg")
-        nc.vector.tensor_scalar(w2_neg[:], w2_sb[:], -1.0, None, MULT)
+        make_identity(nc, ident_f32[:])
 
         window = held.tile([P, S], BF16, name="window")
         for n in range(BLOCKS):
@@ -60,6 +56,8 @@ def tile_gcndeno_kernel(tc, table, lap, w0, w1, w2, b, offs, out):
         nc.tensor.matmul(y1_ps[:], w1_sb[:], looked_up, start=True, stop=True)
         y1_sb = held.tile([P, N], F32, name="y1_sb")
         nc.vector.tensor_copy(y1_sb[:], y1_ps[:])
+        y2_sb = held.tile([P, N], F32, name="y2_sb")
+        nc.vector.tensor_copy(y2_sb[:], y2_ps[:])
 
         flipped = flips.tile([N, P], BF16, name="flipped")
         nc.tensor.transpose(flipped[:], y2x2[:], ident_bf[:])
@@ -73,16 +71,9 @@ def tile_gcndeno_kernel(tc, table, lap, w0, w1, w2, b, offs, out):
         nc.tensor.matmul(zT_ps[:], lap_sb[:], y2x2T[:], start=False, stop=True)
         zT = held.tile([N, P], BF16, name="zT")
         nc.vector.tensor_copy(zT[:], zT_ps[:])
-        for h in range(2):
-            nc.tensor.matmul(
-                acc_ps[:, h * HALF : (h + 1) * HALF],
-                w2_neg[:],
-                window[:].indirect(offsets[:, h * (HALF // 16) : (h + 1) * (HALF // 16)]),
-                start=False,
-                stop=False,
-            )
 
         nc.tensor.matmul(acc_ps[:], zT[:], lap_sb[:], start=False, stop=True)
         result = held.tile([P, N], F32, name="result")
-        nc.vector.tensor_scalar(result[:], acc_ps[:], bias[:, 0:1], 0.0, ADD, MAX)
+        nc.vector.scalar_tensor_tensor(result[:], acc_ps[:], bias[:, 0:1], y2_sb[:], ADD, SUBTRACT)
+        nc.vector.tensor_scalar_max(result[:], result[:], 0.0)
         nc.sync.dma_start(out, result[:])

@@ -5,8 +5,9 @@ P = 128
 S = 512
 BLOCKS = S // P
 N = 128
+HALF = N // 2
 BF16, F32, U16 = mybir.dt.bfloat16, mybir.dt.float32, mybir.dt.uint16
-MULT, ADD, SUBTRACT = mybir.AluOpType.mult, mybir.AluOpType.add, mybir.AluOpType.subtract
+MULT, ADD, MAX = mybir.AluOpType.mult, mybir.AluOpType.add, mybir.AluOpType.max
 
 FLOPS = 2 * P * P * N * 5
 
@@ -27,18 +28,20 @@ def tile_gcndeno_kernel(tc, table, lap, w0, w1, w2, b, offs, out):
         w2_sb = held.tile([P, P], BF16, name="w2_sb")
         nc.scalar.dma_start(w2_sb[:], w2)
         w1_sb = held.tile([P, P], BF16, name="w1_sb")
-        nc.scalar.dma_start(w1_sb[:], w1)
+        nc.sync.dma_start(w1_sb[:], w1)
         w0_sb = held.tile([P, P], BF16, name="w0_sb")
         nc.scalar.dma_start(w0_sb[:], w0)
         lap_sb = held.tile([P, P], BF16, name="lap_sb")
         nc.sync.dma_start(lap_sb[:], lap)
         bias = held.tile([P, 1], F32, name="bias")
-        nc.sync.dma_start(bias[:], b)
+        nc.scalar.dma_start(bias[:], b)
 
         ident_bf = held.tile([P, P], BF16, name="ident_bf")
         make_identity(nc, ident_bf[:])
         ident_f32 = held.tile([P, P], F32, name="ident_f32")
         make_identity(nc, ident_f32[:])
+        w2_neg = held.tile([P, P], BF16, name="w2_neg")
+        nc.gpsimd.tensor_scalar(w2_neg[:], w2_sb[:], -1.0, None, MULT)
 
         window = held.tile([P, S], BF16, name="window")
         for n in range(BLOCKS):
@@ -56,8 +59,6 @@ def tile_gcndeno_kernel(tc, table, lap, w0, w1, w2, b, offs, out):
         nc.tensor.matmul(y1_ps[:], w1_sb[:], looked_up, start=True, stop=True)
         y1_sb = held.tile([P, N], F32, name="y1_sb")
         nc.vector.tensor_copy(y1_sb[:], y1_ps[:])
-        y2_sb = held.tile([P, N], F32, name="y2_sb")
-        nc.vector.tensor_copy(y2_sb[:], y2_ps[:])
 
         flipped = flips.tile([N, P], BF16, name="flipped")
         nc.tensor.transpose(flipped[:], y2x2[:], ident_bf[:])
@@ -71,9 +72,16 @@ def tile_gcndeno_kernel(tc, table, lap, w0, w1, w2, b, offs, out):
         nc.tensor.matmul(zT_ps[:], lap_sb[:], y2x2T[:], start=False, stop=True)
         zT = held.tile([N, P], BF16, name="zT")
         nc.vector.tensor_copy(zT[:], zT_ps[:])
+        for h in range(2):
+            nc.tensor.matmul(
+                acc_ps[:, h * HALF : (h + 1) * HALF],
+                w2_neg[:],
+                window[:].indirect(offsets[:, h * (HALF // 16) : (h + 1) * (HALF // 16)]),
+                start=False,
+                stop=False,
+            )
 
         nc.tensor.matmul(acc_ps[:], zT[:], lap_sb[:], start=False, stop=True)
         result = held.tile([P, N], F32, name="result")
-        nc.vector.scalar_tensor_tensor(result[:], acc_ps[:], bias[:, 0:1], y2_sb[:], ADD, SUBTRACT)
-        nc.vector.tensor_scalar_max(result[:], result[:], 0.0)
+        nc.vector.tensor_scalar(result[:], acc_ps[:], bias[:, 0:1], 0.0, ADD, MAX)
         nc.sync.dma_start(out, result[:])

@@ -7,7 +7,8 @@ BLOCKS = S // P
 N = 128
 HALF = N // 2
 BF16, F32, U16 = mybir.dt.bfloat16, mybir.dt.float32, mybir.dt.uint16
-MULT, ADD, MAX = mybir.AluOpType.mult, mybir.AluOpType.add, mybir.AluOpType.max
+MULT = mybir.AluOpType.mult
+RELU = mybir.ActivationFunctionType.Relu
 
 FLOPS = 2 * P * P * N * 5
 
@@ -35,6 +36,11 @@ def tile_gcndeno_kernel(tc, table, lap, w0, w1, w2, b, offs, out):
         nc.sync.dma_start(lap_sb[:], lap)
         bias = held.tile([P, 1], F32, name="bias")
         nc.scalar.dma_start(bias[:], b)
+
+        cold = held.tile([P, 1], F32, name="cold")
+        nc.vector.memset(cold[:], 0.0)
+        warmed = held.tile([P, 1], F32, name="warmed")
+        nc.scalar.activation(warmed[:], cold[:], RELU)
 
         ident_bf = held.tile([P, P], BF16, name="ident_bf")
         make_identity(nc, ident_bf[:])
@@ -83,5 +89,5 @@ def tile_gcndeno_kernel(tc, table, lap, w0, w1, w2, b, offs, out):
 
         nc.tensor.matmul(acc_ps[:], zT[:], lap_sb[:], start=False, stop=True)
         result = held.tile([P, N], F32, name="result")
-        nc.vector.tensor_scalar(result[:], acc_ps[:], bias[:, 0:1], 0.0, ADD, MAX)
+        nc.scalar.activation(result[:], acc_ps[:], RELU, bias=bias[:, 0:1])
         nc.sync.dma_start(out, result[:])

@@ -67,7 +67,7 @@ def tile_gcndeno_kernel(tc, table, lap, w0, w1, w2, b, offs, out):
         nc.vector.tensor_copy(y1_sb[:], y1_ps[:])
 
         flipped = flips.tile([N, P], BF16, name="flipped")
-        nc.tensor.transpose(flipped[:], y2x2[:], ident_bf[:])
+        nc.tensor.matmul(flipped[:], y2x2[:], ident_bf[:], start=True, stop=True)
         y2x2T = held.tile([N, P], BF16, name="y2x2T")
         nc.vector.tensor_copy(y2x2T[:], flipped[:])
 

@@ -7,7 +7,7 @@ BLOCKS = S // P
 N = 128
 HALF = N // 2
 BF16, F32, U16 = mybir.dt.bfloat16, mybir.dt.float32, mybir.dt.uint16
-MULT = mybir.AluOpType.mult
+MULT, ADD = mybir.AluOpType.mult, mybir.AluOpType.add
 RELU = mybir.ActivationFunctionType.Relu
 
 FLOPS = 2 * P * P * N * 5
@@ -66,18 +66,25 @@ def tile_gcndeno_kernel(tc, table, lap, w0, w1, w2, b, offs, out):
         y1_sb = held.tile([P, N], F32, name="y1_sb")
         nc.vector.tensor_copy(y1_sb[:], y1_ps[:])
 
-        flipped = flips.tile([N, P], BF16, name="flipped")
-        nc.tensor.matmul(flipped[:], y2x2[:], ident_bf[:], start=True, stop=True)
-        y2x2T = held.tile([N, P], BF16, name="y2x2T")
-        nc.vector.tensor_copy(y2x2T[:], flipped[:])
+        halves = [slice(h * HALF, (h + 1) * HALF) for h in range(2)]
+        y2x2T = [held.tile([N, HALF], BF16, name=f"y2x2T{h}") for h in range(2)]
+        for h in range(2):
+            flipped = flips.tile([N, HALF], BF16, name="flipped")
+            nc.tensor.matmul(flipped[:], y2x2[:], ident_bf[:, halves[h]], start=True, stop=True)
+            nc.vector.tensor_copy(y2x2T[h][:], flipped[:])
 
-        zT_ps = psum.tile([N, P], F32, name="zT_ps")
-        nc.tensor.matmul(zT_ps[:], y1_sb[:], ident_f32[:], is_transpose=True, start=True, stop=False)
+        y1T_ps = psum.tile([N, P], F32, name="y1T_ps")
+        nc.tensor.transpose(y1T_ps[:], y1_sb[:], ident_f32[:])
+        y1T = held.tile([N, P], F32, name="y1T")
+        nc.scalar.copy(y1T[:], y1T_ps[:])
+
         acc_ps = psum.tile([P, N], F32, name="acc_ps")
         nc.tensor.matmul(acc_ps[:], w0_sb[:], looked_up, start=True, stop=False)
-        nc.tensor.matmul(zT_ps[:], lap_sb[:], y2x2T[:], start=False, stop=True)
         zT = held.tile([N, P], BF16, name="zT")
-        nc.vector.tensor_copy(zT[:], zT_ps[:])
+        for h in range(2):
+            zT_ps = flips.tile([N, HALF], F32, name="zT_ps", tag="flipped")
+            nc.tensor.matmul(zT_ps[:], lap_sb[:], y2x2T[h][:], start=True, stop=True)
+            nc.vector.tensor_tensor(zT[:, halves[h]], zT_ps[:], y1T[:, halves[h]], ADD)
         for h in range(2):
             nc.tensor.matmul(
                 acc_ps[:, h * HALF : (h + 1) * HALF],

import concourse.mybir as mybir
from concourse.masks import make_identity

P = 128
S = 512
BLOCKS = S // P
N = 128
HALF = N // 2
BF16, F32, U16 = mybir.dt.bfloat16, mybir.dt.float32, mybir.dt.uint16
MULT, ADD = mybir.AluOpType.mult, mybir.AluOpType.add
RELU = mybir.ActivationFunctionType.Relu

FLOPS = 2 * P * P * N * 5


def tile_gcndeno_kernel(tc, table, lap, w0, w1, w2, b, offs, out):
    nc = tc.nc
    with (
        tc.tile_pool(name="held", bufs=1) as held,
        tc.psum_pool(name="psum", bufs=1) as psum,
        tc.psum_pool(name="flips", bufs=BLOCKS) as flips,
    ):
        rows = [held.tile([P, P], BF16, name=f"rows{n}") for n in range(BLOCKS)]
        for n in range(BLOCKS):
            queue = nc.sync if n % 2 == 0 else nc.scalar
            queue.dma_start(rows[n][:], table[n * P : (n + 1) * P, :])
        offsets = held.tile([P, N // 16], U16, name="offsets")
        nc.sync.dma_start(offsets[:], offs)
        w2_sb = held.tile([P, P], BF16, name="w2_sb")
        nc.scalar.dma_start(w2_sb[:], w2)
        w1_sb = held.tile([P, P], BF16, name="w1_sb")
        nc.sync.dma_start(w1_sb[:], w1)
        w0_sb = held.tile([P, P], BF16, name="w0_sb")
        nc.scalar.dma_start(w0_sb[:], w0)
        lap_sb = held.tile([P, P], BF16, name="lap_sb")
        nc.sync.dma_start(lap_sb[:], lap)
        bias = held.tile([P, 1], F32, name="bias")
        nc.scalar.dma_start(bias[:], b)

        cold = held.tile([P, 1], F32, name="cold")
        nc.vector.memset(cold[:], 0.0)
        warmed = held.tile([P, 1], F32, name="warmed")
        nc.scalar.activation(warmed[:], cold[:], RELU)

        ident_bf = held.tile([P, P], BF16, name="ident_bf")
        make_identity(nc, ident_bf[:])
        ident_f32 = held.tile([P, P], F32, name="ident_f32")
        make_identity(nc, ident_f32[:])
        w2_neg = held.tile([P, P], BF16, name="w2_neg")
        nc.gpsimd.tensor_scalar(w2_neg[:], w2_sb[:], -1.0, None, MULT)

        window = held.tile([P, S], BF16, name="window")
        for n in range(BLOCKS):
            flipped = flips.tile([P, P], BF16, name="flipped")
            nc.tensor.transpose(flipped[:], rows[n][:], ident_bf[:])
            nc.vector.tensor_copy(window[:, n * P : (n + 1) * P], flipped[:])

        looked_up = window[:].indirect(offsets[:])
        y2_ps = psum.tile([P, N], F32, name="y2_ps")
        nc.tensor.matmul(y2_ps[:], w2_sb[:], looked_up, start=True, stop=True)
        y2x2 = held.tile([P, N], BF16, name="y2x2")
        nc.vector.tensor_scalar(y2x2[:], y2_ps[:], 2.0, None, MULT)

        y1_ps = psum.tile([P, N], F32, name="y1_ps")
        nc.tensor.matmul(y1_ps[:], w1_sb[:], looked_up, start=True, stop=True)
        y1_sb = held.tile([P, N], F32, name="y1_sb")
        nc.vector.tensor_copy(y1_sb[:], y1_ps[:])

        halves = [slice(h * HALF, (h + 1) * HALF) for h in range(2)]
        y2x2T = [held.tile([N, HALF], BF16, name=f"y2x2T{h}") for h in range(2)]
        for h in range(2):
            flipped = flips.tile([N, HALF], BF16, name="flipped")
            nc.tensor.matmul(flipped[:], y2x2[:], ident_bf[:, halves[h]], start=True, stop=True)
            nc.vector.tensor_copy(y2x2T[h][:], flipped[:])

        y1T_ps = psum.tile([N, P], F32, name="y1T_ps")
        nc.tensor.transpose(y1T_ps[:], y1_sb[:], ident_f32[:])
        y1T = held.tile([N, P], F32, name="y1T")
        nc.scalar.copy(y1T[:], y1T_ps[:])

        acc_ps = psum.tile([P, N], F32, name="acc_ps")
        nc.tensor.matmul(acc_ps[:], w0_sb[:], looked_up, start=True, stop=False)
        zT = held.tile([N, P], BF16, name="zT")
        for h in range(2):
            zT_ps = flips.tile([N, HALF], F32, name="zT_ps", tag="flipped")
            nc.tensor.matmul(zT_ps[:], lap_sb[:], y2x2T[h][:], start=True, stop=True)
            nc.vector.tensor_tensor(zT[:, halves[h]], zT_ps[:], y1T[:, halves[h]], ADD)
        for h in range(2):
            nc.tensor.matmul(
                acc_ps[:, h * HALF : (h + 1) * HALF],
                w2_neg[:],
                window[:].indirect(offsets[:, h * (HALF // 16) : (h + 1) * (HALF // 16)]),
                start=False,
                stop=False,
            )

        nc.tensor.matmul(acc_ps[:], zT[:], lap_sb[:], start=False, stop=True)
        result = held.tile([P, N], F32, name="result")
        nc.scalar.activation(result[:], acc_ps[:], RELU, bias=bias[:, 0:1])
        nc.sync.dma_start(out, result[:])
